import numpy as np
import ml_dtypes


def mxq(x, axis, fmt="e4m3"):
    dtype, down = {"e4m3": (ml_dtypes.float8_e4m3fn, 7), "e5m2": (ml_dtypes.float8_e5m2, 14)}[fmt]
    v = np.moveaxis(np.asarray(x, np.float32).astype(ml_dtypes.bfloat16).astype(np.float64), axis, -1)
    blocks = v.reshape(v.shape[:-1] + (-1, 32))
    amax = np.abs(blocks).max(-1, keepdims=True)
    byte = np.maximum(np.where(amax > 0, np.frexp(amax)[1] - 1 + 127, 0) - down, 1)
    scale = np.exp2(byte - 127.0)
    codes = (blocks / scale).astype(np.float32).astype(dtype).astype(np.float64)
    return np.moveaxis((codes * scale).reshape(v.shape), -1, axis)


WIDE = False


def mx_kscale(k):
    if not WIDE:
        return np.ones(k)
    levels = np.array([10, -10, 5, -5, 0])
    if k % 512:
        return np.exp2(np.random.permutation(np.resize(levels, k // 32))).repeat(32)
    a = np.empty((k // 512, 16))
    for p in range(k // 512):
        a[p, :8] = np.random.permutation(np.resize(levels, 8))
        for g in range(8):
            far = levels[np.abs(levels - a[p, g]) >= 10]
            a[p, g + 8] = far[np.random.randint(len(far))]
    return np.exp2(a.ravel()).repeat(32)


BF16 = ml_dtypes.bfloat16


def bf(x):
    return np.asarray(x, np.float32).astype(BF16)


def f64(x):
    return np.asarray(x).astype(np.float64)


E2M1 = np.array([0.0, 0.5, 1.0, 1.5, 2.0, 3.0, 4.0, 6.0, -0.0, -0.5, -1.0, -1.5, -2.0, -3.0, -4.0, -6.0])


def pack_weight(w, fmt):
    k, n = w.shape
    w = f64(bf(w)).reshape(k // 32, 32, n)
    amax = np.abs(w).max(1)
    if fmt == "e4m3":
        byte = np.frexp(amax)[1] - 1 + 127 - 7
    else:
        mant, ex = np.frexp(amax / 6.0)
        byte = np.where(mant > 0.5, ex, ex - 1) + 127
    byte = np.clip(np.where(amax > 0, byte, 1), 1, 254)
    scaled = (w * np.exp2(127.0 - byte)[:, None, :]).reshape(k, n).astype(np.float32)
    by_word = np.ascontiguousarray(scaled.reshape(k // 512, 128, 4, n).transpose(0, 1, 3, 2))
    if fmt == "e4m3":
        words = by_word.astype(ml_dtypes.float8_e4m3fn).view(np.uint8)
    else:
        c = by_word.astype(ml_dtypes.float4_e2m1fn).view(np.uint8) & 0xF
        words = c[..., 0::2] | (c[..., 1::2] << 4)
    return np.ascontiguousarray(words), np.ascontiguousarray(byte.astype(np.uint8).reshape(k // 512, 16, n))


def unpack_weight(words, scales, fmt):
    g, p, n, _ = words.shape
    if fmt == "e4m3":
        vals = np.ascontiguousarray(words).view(ml_dtypes.float8_e4m3fn).astype(np.float64)
    else:
        nib = np.empty((g, p, n, 4), np.uint8)
        nib[..., 0::2] = words & 0xF
        nib[..., 1::2] = words >> 4
        vals = E2M1[nib]
    vals = vals * np.repeat(np.exp2(scales.astype(np.float64) - 127.0), 8, axis=1)[..., None]
    return vals.transpose(0, 1, 3, 2).reshape(g * 512, n)


B, D, MP, MID, L = 4096, 768, 512, 1024, 4
HALF = D // 2


def draw0():
    s = mx_kscale(MP)
    t = mx_kscale(MID)
    x = bf(np.random.standard_normal((B, D)))
    h_prev = bf(np.maximum(np.random.standard_normal((B, MP)) * np.sqrt(2.0), 0.0) * s)
    w_hid_words, w_hid_scales = pack_weight(np.random.standard_normal((MP, MID)) * np.sqrt(2.0 / MP) / s[:, None] * t, "e4m3")
    b_hid = bf(np.random.standard_normal(MID) * 0.2 * t)
    w_out_words, w_out_scales = pack_weight(np.random.standard_normal((MID, HALF)) / np.sqrt(MID) / t[:, None], "e4m3")
    b_out = bf(np.random.standard_normal(HALF) * 0.2)
    return {
        "x": x,
        "h_prev": h_prev,
        "w_hid_words": w_hid_words,
        "w_hid_scales": w_hid_scales,
        "b_hid": b_hid,
        "w_out_words": w_out_words,
        "w_out_scales": w_out_scales,
        "b_out": b_out,
    }


def core(x, h_prev, w_hid_words, w_hid_scales, b_hid, w_out_words, w_out_scales, b_out):
    x = f64(x)
    first = x[:, 0::2]
    second = x[:, 1::2]
    h = np.maximum((mxq(f64(h_prev), 1, "e4m3") @ unpack_weight(w_hid_words, w_hid_scales, "e4m3")) + f64(b_hid), 0.0)
    shift = (mxq(h, 1, "e4m3") @ unpack_weight(w_out_words, w_out_scales, "e4m3")) + f64(b_out)
    y_second = second + shift
    return np.stack([first, y_second], axis=2).reshape(x.shape)


def e4m3fn_bytes(y):
    return np.clip(np.asarray(y, np.float64), -448.0, 448.0).astype(np.float32).astype(ml_dtypes.float8_e4m3fn).view(np.uint8)


def e4m3fn_values(b):
    return np.asarray(b, np.uint8).view(ml_dtypes.float8_e4m3fn).astype(np.float64)


def setup_inputs():
    d = draw0()
    x0 = np.asarray(d['h_prev']).astype(np.float64)
    s = (np.max(np.abs(x0), axis=(0,), keepdims=True) / 448.0).astype(np.float32)
    out = {}
    for k, v in d.items():
        if k == 'h_prev':
            out['h_prev_bytes'] = e4m3fn_bytes(x0 / s.astype(np.float64))
            out['h_prev_scale'] = s
        else:
            out[k] = v
    return out


def reference(x, h_prev_bytes, h_prev_scale, w_hid_words, w_hid_scales, b_hid, w_out_words, w_out_scales, b_out):
    return core(x, e4m3fn_values(h_prev_bytes) * h_prev_scale.astype(np.float64), w_hid_words, w_hid_scales, b_hid, w_out_words, w_out_scales, b_out)

@@ -1,0 +1,299 @@
+from contextlib import ExitStack
+
+import concourse.mybir as mybir
+from concourse.masks import make_identity
+
+B, D, MP, MID = 4096, 768, 512, 1024
+HALF = D // 2
+FLOPS = 2 * B * (MP * MID + MID * HALF)
+
+F32 = mybir.dt.float32
+BF16 = mybir.dt.bfloat16
+U8 = mybir.dt.uint8
+I32 = mybir.dt.int32
+U32 = mybir.dt.uint32
+FP8 = mybir.dt.float8_e4m3fn
+FP8X4 = mybir.dt.float8_e4m3fn_x4
+ADD = mybir.AluOpType.add
+MULT = mybir.AluOpType.mult
+RELU = mybir.ActivationFunctionType.Relu
+IDENTITY = mybir.ActivationFunctionType.Identity
+
+P = 128
+TOK = 512
+SUB = TOK // P
+GROUPS = B // TOK
+MIX = 2
+N_SCALAR = 96
+
+
+def tile_additivecoupling_pa_t_w8_kernel(
+    tc, x, h_prev_bytes, h_prev_scale, w_hid_words, w_hid_scales, b_hid, w_out_words, w_out_scales, b_out, out
+):
+    nc = tc.nc
+    with ExitStack() as ctx:
+        keep = ctx.enter_context(tc.tile_pool(name="keep", bufs=1))
+        pool = ctx.enter_context(tc.tile_pool(name="pool", bufs=2))
+        rot = ctx.enter_context(tc.psum_pool(name="rot", bufs=6))
+        fixed = ctx.enter_context(tc.psum_pool(name="fixed", bufs=1))
+        ctx.enter_context(tc.manual_schedule())
+
+        codes_in = [keep.tile([P, SUB * MP], U8, name="codes_in%d" % g, align_bytes=64) for g in range(GROUPS)]
+        x_in = [keep.tile([P, SUB, D], BF16, name="x_in%d" % g) for g in range(GROUPS)]
+        k_scale = keep.tile([P, 2, MP], F32)
+        wh_raw = keep.tile([P, MID], I32)
+        wh_scale_raw = keep.tile([P, MID], U8, align_bytes=64)
+        wh = keep.tile([P, MID], I32, align_bytes=64)
+        wh_scale = keep.tile([P, MID], U8, align_bytes=64)
+        wo = keep.tile([P, 2, HALF], I32, align_bytes=64)
+        wo_scale = keep.tile([P, 2, HALF], U8, align_bytes=64)
+        bh = keep.tile([P, 2, 4], BF16)
+        bo = keep.tile([P, 3, 2], BF16)
+        zeros = keep.tile([P, 256], BF16)
+        ident = keep.tile([P, P], F32)
+        warm = keep.tile([P, 1], F32)
+
+        nc.vector.memset(wh_scale_raw[:].bitcast(I32), 0)
+        nc.vector.memset(wo_scale[:].rearrange("p g n -> p (g n)").bitcast(I32), 0)
+        nc.vector.memset(zeros[:], 0.0)
+        nc.vector.memset(warm[:], 0.0)
+        make_identity(nc, ident[:])
+
+        def load_codes(g):
+            nc.sync.dma_start(out=codes_in[g][:], in_=h_prev_bytes[g * TOK : (g + 1) * TOK, :].rearrange("(p j) k -> p (j k)", j=SUB))
+
+        def load_x(g):
+            nc.sync.dma_start(
+                out=x_in[g][:].rearrange("p j d -> p (j d)"), in_=x[g * TOK : (g + 1) * TOK, :].rearrange("(p j) d -> p (j d)", j=SUB)
+            )
+
+        nc.scalar.dma_start(out=k_scale[:, 0, :], in_=h_prev_scale.rearrange("o k -> (o k)").partition_broadcast(P))
+        nc.scalar.dma_start(out=bh[:], in_=b_hid.rearrange("(h p t) -> p h t", h=2, t=4))
+        nc.scalar.dma_start(out=bo[:, :, 0:1], in_=b_out.rearrange("(c p o) -> p c o", p=P, o=1))
+        load_codes(0)
+        load_codes(1)
+        for q in range(4):
+            nc.sync.dma_start(
+                out=wh_scale_raw[32 * q : 32 * q + 4, :].bitcast(I32), in_=w_hid_scales[0][4 * q : 4 * q + 4, :].bitcast(I32)
+            )
+        nc.sync.dma_start(out=wh_raw[:], in_=w_hid_words[0].rearrange("p n t -> p (n t)").bitcast(I32))
+        load_codes(2)
+        load_codes(3)
+        for q in range(4):
+            for g in range(2):
+                nc.sync.dma_start(
+                    out=wo_scale[32 * q : 32 * q + 4, g, :].bitcast(I32), in_=w_out_scales[g][4 * q : 4 * q + 4, :].bitcast(I32)
+                )
+        for g in range(2):
+            nc.sync.dma_start(out=wo[:, g, :], in_=w_out_words[g].rearrange("p n t -> p (n t)").bitcast(I32))
+        load_x(0)
+        for g in range(4, GROUPS):
+            load_codes(g)
+            load_x(g - 3)
+        for g in range(GROUPS - 3, GROUPS):
+            load_x(g)
+
+        nc.scalar.activation(out=warm[:], in_=warm[:], func=RELU)
+
+        mix = [fixed.tile([P, 512], F32, name="mix%d" % d) for d in range(MIX)]
+        for d in range(MIX):
+            nc.tensor.matmul(out=mix[d][:, 0:256], lhsT=zeros[:, 0:P], rhs=zeros[:], start=True, stop=True)
+
+        def new_bank():
+            bank = rot.tile([P, 512], F32)
+            return bank
+
+        hb, grouped, xc, xs = {}, {}, {}, {}
+        hp, hg, hc, hs, st, yo = {}, {}, {}, {}, {}, {}
+
+        def widen(g, half):
+            if not 0 <= g < GROUPS:
+                return
+            if g not in hb:
+                h_bf = pool.tile([P, SUB * MP], BF16, bufs=6)
+                hb[g] = h_bf
+            if g == 0:
+                for j in (2 * half, 2 * half + 1):
+                    cols = slice(j * MP, (j + 1) * MP)
+                    nc.vector.tensor_tensor(out=hb[g][:, cols], in0=codes_in[g][:, cols].bitcast(FP8), in1=k_scale[:, 0, :], op=MULT)
+                return
+            cols = slice(half * 2 * MP, (half + 1) * 2 * MP)
+            nc.vector.tensor_tensor(
+                out=hb[g][:, cols], in0=codes_in[g][:, cols].bitcast(FP8), in1=k_scale[:].rearrange("p a k -> p (a k)"), op=MULT
+            )
+
+        def turn(g, half):
+            if not 0 <= g < GROUPS:
+                return
+            if g not in grouped:
+                h_grouped = pool.tile([P, TOK * 4], BF16, align_bytes=64)
+                grouped[g] = h_grouped
+            bank = new_bank()
+            for j in range(2):
+                words = hb[g][:, (2 * half + j) * MP : (2 * half + j + 1) * MP].bitcast(F32)
+                for u in range(2):
+                    c = (2 * j + u) * P
+                    nc.tensor.transpose(bank[:, c : c + P], words[:, u : MP // 2 : 2], ident[:])
+            dst = grouped[g][:, half * 1024 : (half + 1) * 1024].bitcast(F32)
+            nc.scalar.copy(
+                out=dst.rearrange("p (j r u) -> p j r u", j=2, u=2), in_=bank[:].rearrange("p (j u r) -> p j r u", j=2, u=2)
+            )
+
+        def quant_x(g):
+            if not 0 <= g < GROUPS:
+                return
+            x_codes = pool.tile([P, TOK], U32, align_bytes=64)
+            x_scales = pool.tile([P, TOK], U8, align_bytes=64)
+            xc[g], xs[g] = x_codes, x_scales
+            nc.vector.quantize_mx(out=x_codes[:].bitcast(FP8X4), scales=x_scales[:], in_=grouped[g][:])
+
+        def first(g, half, t):
+            if not 0 <= g < GROUPS:
+                return
+            if (g, half) not in hp:
+                h_planes = pool.tile([P, 4, TOK], BF16, bufs=3)
+                hp[g, half] = h_planes
+            bank = new_bank()
+            m = slice((4 * half + t) * P, (4 * half + t + 1) * P)
+            nc.tensor.matmul_mx(
+                out=bank[:],
+                lhsT=wh[:, m].bitcast(FP8X4),
+                lhsT_scale=wh_scale[:, m],
+                rhs=xc[g][:].bitcast(FP8X4),
+                rhs_scale=xs[g][:],
+                start=True,
+                stop=True,
+            )
+            nc.scalar.activation(out=hp[g, half][:, t, :], in_=bank[:], func=RELU, bias=bh[:, half, t : t + 1])
+
+        def weave(g, half, on_scalar):
+            if not 0 <= g < GROUPS:
+                return
+            if (g, half) not in hg:
+                h_grp = pool.tile([P, TOK, 4], BF16, bufs=3, align_bytes=64)
+                hg[g, half] = h_grp
+            cols = slice(0, N_SCALAR) if on_scalar else slice(N_SCALAR, TOK)
+            dst = hg[g, half][:, cols, :].rearrange("p (c i) t -> p c t i", i=4)
+            src = hp[g, half][:, :, cols].rearrange("p t (c i) -> p c t i", i=4)
+            if on_scalar:
+                nc.scalar.copy(out=dst, in_=src)
+            else:
+                nc.vector.tensor_copy(out=dst, in_=src)
+
+        def quant_h(g, half):
+            if not 0 <= g < GROUPS:
+                return
+            h_codes = pool.tile([P, TOK], U32, bufs=4, align_bytes=64)
+            h_scales = pool.tile([P, TOK], U8, bufs=4, align_bytes=64)
+            hc[g, half], hs[g, half] = h_codes, h_scales
+            nc.vector.quantize_mx(
+                out=h_codes[:].bitcast(FP8X4), scales=h_scales[:], in_=hg[g, half][:].rearrange("p n t -> p (n t)")
+            )
+
+        def second(g, c):
+            if not 0 <= g < GROUPS:
+                return
+            if g not in st:
+                shift_t = pool.tile([P, 3, TOK], F32)
+                st[g] = shift_t
+            bank = new_bank()
+            for half in range(2):
+                nc.tensor.matmul_mx(
+                    out=bank[:],
+                    lhsT=wo[:, half, c * P : (c + 1) * P].bitcast(FP8X4),
+                    lhsT_scale=wo_scale[:, half, c * P : (c + 1) * P],
+                    rhs=hc[g, half][:].bitcast(FP8X4),
+                    rhs_scale=hs[g, half][:],
+                    start=(half == 0),
+                    stop=(half == 1),
+                )
+            nc.scalar.activation(out=st[g][:, c, :], in_=bank[:], func=IDENTITY, bias=bo[:, c, 0:1])
+
+        uses = []
+        for pair in range(2):
+            a, b = 2 * pair, 2 * pair + 1
+            uses.append(((a, 0), (a, 1)))
+            uses.append(((a, 2), (b, 2)))
+            uses.append(((b, 0), (b, 1)))
+
+        def turn_back(g, n):
+            if not 0 <= g < GROUPS:
+                return
+            for s in range(2):
+                j, c = uses[n][s]
+                nc.tensor.transpose(
+                    mix[n % MIX][:, 256 + s * P : 256 + (s + 1) * P], st[g][:, c, j * P : (j + 1) * P], ident[:]
+                )
+
+        def couple(g, n):
+            if not 0 <= g < GROUPS:
+                return
+            pair = n // 3
+            if n % 3 == 0:
+                y_pair = pool.tile([P, 2, D], F32, bufs=3)
+                yo[g, pair] = y_pair
+            y = yo[g, pair]
+            xi = x_in[g][:, 2 * pair : 2 * pair + 2, :]
+            bank = mix[n % MIX]
+            if n % 3 == 1:
+                nc.vector.tensor_tensor(
+                    out=y[:, :, 512:768].rearrange("p q (n e) -> p q n e", e=2),
+                    in0=bank[:].rearrange("p (e q n) -> p q n e", e=2, q=2),
+                    in1=xi[:, :, 512:768].rearrange("p q (n e) -> p q n e", e=2),
+                    op=ADD,
+                )
+            else:
+                q = 0 if n % 3 == 0 else 1
+                nc.vector.tensor_tensor(
+                    out=y[:, q, 0:512].rearrange("p (n e) -> p n e", e=2),
+                    in0=bank[:].rearrange("p (e n) -> p n e", e=2),
+                    in1=xi[:, q, 0:512].rearrange("p (n e) -> p n e", e=2),
+                    op=ADD,
+                )
+            if n % 3 == 2:
+                rows = out[g * TOK : (g + 1) * TOK, :].rearrange("(p j) d -> p j d", j=SUB)
+                nc.sync.dma_start(out=rows[:, 2 * pair : 2 * pair + 2, :], in_=y[:])
+
+        def prepare(g):
+            if g != 0:
+                return
+            nc.vector.tensor_copy(out=k_scale[:, 1, :], in_=k_scale[:, 0, :])
+            nc.vector.tensor_copy(out=wh_scale[:].rearrange("p (h t m) -> p h t m", h=2, t=4), in_=wh_scale_raw[:].rearrange("p (h m t) -> p h t m", h=2, t=4))
+            nc.vector.tensor_copy(out=wh[:].rearrange("p (h t m) -> p h t m", h=2, t=4), in_=wh_raw[:].rearrange("p (h m t) -> p h t m", h=2, t=4))
+
+        for i in range(-6, GROUPS + 4):
+            first(i, 0, 0)
+            first(i, 0, 1)
+            first(i, 0, 2)
+            first(i, 0, 3)
+            first(i, 1, 0)
+            widen(i + 4, 0)
+            turn_back(i - 2, 0)
+            turn_back(i - 2, 1)
+            first(i, 1, 3)
+            second(i - 1, 0)
+            first(i, 1, 1)
+            couple(i - 2, 0)
+            turn_back(i - 2, 2)
+            turn(i + 2, 1)
+            couple(i - 2, 1)
+            first(i, 1, 2)
+            weave(i, 0, True)
+            couple(i - 2, 2)
+            weave(i, 1, True)
+            weave(i, 0, False)
+            turn_back(i - 2, 3)
+            second(i - 1, 1)
+            couple(i - 2, 3)
+            turn_back(i - 2, 4)
+            turn_back(i - 2, 5)
+            couple(i - 2, 4)
+            quant_x(i + 2)
+            couple(i - 2, 5)
+            weave(i, 1, False)
+            turn(i + 3, 0)
+            widen(i + 4, 1)
+            prepare(i + 4)
+            second(i - 1, 2)
+            quant_h(i, 0)
+            quant_h(i, 1)

@@ -10,8 +10,8 @@ FLOPS = 2 * B * (MP * MID + MID * HALF)
 F32 = mybir.dt.float32
 BF16 = mybir.dt.bfloat16
 U8 = mybir.dt.uint8
-I32 = mybir.dt.int32
 U32 = mybir.dt.uint32
+I32 = mybir.dt.int32
 FP8 = mybir.dt.float8_e4m3fn
 FP8X4 = mybir.dt.float8_e4m3fn_x4
 ADD = mybir.AluOpType.add
@@ -20,11 +20,15 @@ RELU = mybir.ActivationFunctionType.Relu
 IDENTITY = mybir.ActivationFunctionType.Identity
 
 P = 128
-TOK = 512
-SUB = TOK // P
-GROUPS = B // TOK
-MIX = 2
-N_SCALAR = 96
+PACK = 4
+SUBS = [2, 4, 4, 4, 4, 4, 4, 4, 2]
+FIRST_TOKEN = [P * sum(SUBS[:g]) for g in range(len(SUBS))]
+GROUPS = len(SUBS)
+C_TILES = HALF // P
+COUPLE_BANKS = 3
+WORK_BANKS = 8 - COUPLE_BANKS
+SCALAR_COLUMNS = [64, 128, 128, 128, 128, 128, 128, 128, 96]
+LOOKAHEAD = 3
 
 
 def tile_additivecoupling_pa_t_w8_kernel(
@@ -34,266 +38,266 @@ def tile_additivecoupling_pa_t_w8_kernel(
     with ExitStack() as ctx:
         keep = ctx.enter_context(tc.tile_pool(name="keep", bufs=1))
         pool = ctx.enter_context(tc.tile_pool(name="pool", bufs=2))
-        rot = ctx.enter_context(tc.psum_pool(name="rot", bufs=6))
+        work = ctx.enter_context(tc.psum_pool(name="work", bufs=WORK_BANKS))
         fixed = ctx.enter_context(tc.psum_pool(name="fixed", bufs=1))
         ctx.enter_context(tc.manual_schedule())
 
-        codes_in = [keep.tile([P, SUB * MP], U8, name="codes_in%d" % g, align_bytes=64) for g in range(GROUPS)]
-        x_in = [keep.tile([P, SUB, D], BF16, name="x_in%d" % g) for g in range(GROUPS)]
-        k_scale = keep.tile([P, 2, MP], F32)
-        wh_raw = keep.tile([P, MID], I32)
-        wh_scale_raw = keep.tile([P, MID], U8, align_bytes=64)
-        wh = keep.tile([P, MID], I32, align_bytes=64)
-        wh_scale = keep.tile([P, MID], U8, align_bytes=64)
-        wo = keep.tile([P, 2, HALF], I32, align_bytes=64)
-        wo_scale = keep.tile([P, 2, HALF], U8, align_bytes=64)
-        bh = keep.tile([P, 2, 4], BF16)
-        bo = keep.tile([P, 3, 2], BF16)
+        h_bytes = [keep.tile([P, SUBS[g] * MP], U8, name="h_bytes%d" % g, align_bytes=64) for g in range(GROUPS)]
+        x_rows = [keep.tile([P, SUBS[g], D], BF16, name="x_rows%d" % g) for g in range(GROUPS)]
+        k_column = keep.tile([P, PACK], F32)
+        k_scale = keep.tile([P, max(SUBS), MP], F32)
+        hid_words = keep.tile([P, MID], I32)
+        hid_bytes = keep.tile([P, MID], U8, align_bytes=64)
+        hid_codes = keep.tile([P, MID], I32, align_bytes=64)
+        hid_scales = keep.tile([P, MID], U8, align_bytes=64)
+        out_codes = keep.tile([P, 2, HALF], I32, align_bytes=64)
+        out_scales = keep.tile([P, 2, HALF], U8, align_bytes=64)
+        hid_bias = keep.tile([P, 2, PACK], BF16)
+        out_bias = keep.tile([P, C_TILES, 2], BF16)
         zeros = keep.tile([P, 256], BF16)
-        ident = keep.tile([P, P], F32)
-        warm = keep.tile([P, 1], F32)
+        identity = keep.tile([P, P], F32)
 
-        nc.vector.memset(wh_scale_raw[:].bitcast(I32), 0)
-        nc.vector.memset(wo_scale[:].rearrange("p g n -> p (g n)").bitcast(I32), 0)
-        nc.vector.memset(zeros[:], 0.0)
-        nc.vector.memset(warm[:], 0.0)
-        make_identity(nc, ident[:])
+        def rows_of(tensor, g):
+            n = SUBS[g] * P
+            return tensor[FIRST_TOKEN[g] : FIRST_TOKEN[g] + n, :].rearrange("(p r) d -> p r d", r=SUBS[g])
 
-        def load_codes(g):
-            nc.sync.dma_start(out=codes_in[g][:], in_=h_prev_bytes[g * TOK : (g + 1) * TOK, :].rearrange("(p j) k -> p (j k)", j=SUB))
+        def load_bytes(g):
+            nc.sync.dma_start(out=h_bytes[g][:], in_=rows_of(h_prev_bytes, g).rearrange("p r k -> p (r k)"))
 
         def load_x(g):
-            nc.sync.dma_start(
-                out=x_in[g][:].rearrange("p j d -> p (j d)"), in_=x[g * TOK : (g + 1) * TOK, :].rearrange("(p j) d -> p (j d)", j=SUB)
-            )
+            nc.sync.dma_start(out=x_rows[g][:], in_=rows_of(x, g))
 
-        nc.scalar.dma_start(out=k_scale[:, 0, :], in_=h_prev_scale.rearrange("o k -> (o k)").partition_broadcast(P))
-        nc.scalar.dma_start(out=bh[:], in_=b_hid.rearrange("(h p t) -> p h t", h=2, t=4))
-        nc.scalar.dma_start(out=bo[:, :, 0:1], in_=b_out.rearrange("(c p o) -> p c o", p=P, o=1))
-        load_codes(0)
-        load_codes(1)
-        for q in range(4):
-            nc.sync.dma_start(
-                out=wh_scale_raw[32 * q : 32 * q + 4, :].bitcast(I32), in_=w_hid_scales[0][4 * q : 4 * q + 4, :].bitcast(I32)
-            )
-        nc.sync.dma_start(out=wh_raw[:], in_=w_hid_words[0].rearrange("p n t -> p (n t)").bitcast(I32))
-        load_codes(2)
-        load_codes(3)
-        for q in range(4):
-            for g in range(2):
+        def load_words(tile_view, words):
+            nc.sync.dma_start(out=tile_view, in_=words.rearrange("p n t -> p (n t)").bitcast(I32))
+
+        def load_scales(tile_view, scales):
+            for q in range(4):
                 nc.sync.dma_start(
-                    out=wo_scale[32 * q : 32 * q + 4, g, :].bitcast(I32), in_=w_out_scales[g][4 * q : 4 * q + 4, :].bitcast(I32)
+                    out=tile_view[32 * q : 32 * q + 4, :].bitcast(I32), in_=scales[4 * q : 4 * q + 4, :].bitcast(I32)
                 )
+
+        nc.vector.memset(hid_bytes[:].bitcast(I32), 0)
+        nc.vector.memset(out_scales[:].rearrange("p g n -> p (g n)").bitcast(I32), 0)
+        nc.vector.memset(zeros[:], 0.0)
+        make_identity(nc, identity[:])
+
+        nc.scalar.dma_start(out=k_column[:], in_=h_prev_scale.rearrange("o (p t) -> p (o t)", t=PACK))
+        nc.scalar.dma_start(out=hid_bias[:], in_=b_hid.rearrange("(h p t) -> p h t", h=2, t=PACK))
+        nc.scalar.dma_start(out=out_bias[:, :, 0:1], in_=b_out.rearrange("(c p o) -> p c o", p=P, o=1))
+        load_bytes(0)
+        load_bytes(1)
+        load_scales(hid_bytes, w_hid_scales[0])
+        load_words(hid_words[:], w_hid_words[0])
+        load_bytes(2)
+        load_bytes(3)
         for g in range(2):
-            nc.sync.dma_start(out=wo[:, g, :], in_=w_out_words[g].rearrange("p n t -> p (n t)").bitcast(I32))
-        load_x(0)
-        for g in range(4, GROUPS):
-            load_codes(g)
-            load_x(g - 3)
-        for g in range(GROUPS - 3, GROUPS):
+            load_scales(out_scales[:, g, :], w_out_scales[g])
+        for g in range(2):
+            load_words(out_codes[:, g, :], w_out_words[g])
+        for g in range(GROUPS):
             load_x(g)
+            if g + LOOKAHEAD + 1 < GROUPS:
+                load_bytes(g + LOOKAHEAD + 1)
 
-        nc.scalar.activation(out=warm[:], in_=warm[:], func=RELU)
+        couple_banks = [fixed.tile([P, 512], F32, name="couple_bank%d" % d) for d in range(COUPLE_BANKS)]
+        for bank in couple_banks:
+            nc.tensor.matmul(out=bank[:, 0:256], lhsT=zeros[:, 0:P], rhs=zeros[:], start=True, stop=True)
 
-        mix = [fixed.tile([P, 512], F32, name="mix%d" % d) for d in range(MIX)]
-        for d in range(MIX):
-            nc.tensor.matmul(out=mix[d][:, 0:256], lhsT=zeros[:, 0:P], rhs=zeros[:], start=True, stop=True)
-
-        def new_bank():
-            bank = rot.tile([P, 512], F32)
+        def work_bank():
+            bank = work.tile([P, 512], F32)
             return bank
 
-        hb, grouped, xc, xs = {}, {}, {}, {}
-        hp, hg, hc, hs, st, yo = {}, {}, {}, {}, {}, {}
+        scale_bank = work_bank()
+        for t in range(PACK):
+            nc.tensor.transpose(scale_bank[:, t * P : (t + 1) * P], k_column[:, t : t + 1].to_broadcast([P, P]), identity[:])
+        for r in range(max(SUBS)):
+            copy = nc.vector.tensor_copy if r == 0 else nc.scalar.copy
+            copy(out=k_scale[:, r, :].rearrange("p (n t) -> p n t", t=PACK), in_=scale_bank[:].rearrange("p (t n) -> p n t", t=PACK))
 
-        def widen(g, half):
-            if not 0 <= g < GROUPS:
-                return
-            if g not in hb:
-                h_bf = pool.tile([P, SUB * MP], BF16, bufs=6)
-                hb[g] = h_bf
-            if g == 0:
-                for j in (2 * half, 2 * half + 1):
-                    cols = slice(j * MP, (j + 1) * MP)
-                    nc.vector.tensor_tensor(out=hb[g][:, cols], in0=codes_in[g][:, cols].bitcast(FP8), in1=k_scale[:, 0, :], op=MULT)
-                return
-            cols = slice(half * 2 * MP, (half + 1) * 2 * MP)
-            nc.vector.tensor_tensor(
-                out=hb[g][:, cols], in0=codes_in[g][:, cols].bitcast(FP8), in1=k_scale[:].rearrange("p a k -> p (a k)"), op=MULT
-            )
+        h_prev, h_prev_quads, h_prev_codes, h_prev_scales = {}, {}, {}, {}
+        h_planes, h_quads, h_codes, h_scales, shift, y = {}, {}, {}, {}, {}, {}
 
-        def turn(g, half):
-            if not 0 <= g < GROUPS:
+        def widen(g):
+            width = SUBS[g] * MP
+            h_wide = pool.tile([P, width], BF16, bufs=4)
+            h_prev[g] = h_wide
+            step = MP if g == 0 else width
+            for c in range(0, width, step):
+                nc.vector.tensor_tensor(
+                    out=h_wide[:, c : c + step],
+                    in0=h_bytes[g][:, c : c + step].bitcast(FP8),
+                    in1=k_scale[:].rearrange("p r k -> p (r k)")[:, 0:step],
+                    op=MULT,
+                )
+
+        def turn(g, pair):
+            if not 0 <= g < GROUPS or 2 * pair >= SUBS[g]:
                 return
-            if g not in grouped:
-                h_grouped = pool.tile([P, TOK * 4], BF16, align_bytes=64)
-                grouped[g] = h_grouped
-            bank = new_bank()
-            for j in range(2):
-                words = hb[g][:, (2 * half + j) * MP : (2 * half + j + 1) * MP].bitcast(F32)
+            if g not in h_prev_quads:
+                quads = pool.tile([P, SUBS[g] * P * PACK], BF16, align_bytes=64)
+                h_prev_quads[g] = quads
+            bank = work_bank()
+            for r in range(2):
+                words = h_prev[g][:, (2 * pair + r) * MP : (2 * pair + r + 1) * MP].bitcast(F32)
                 for u in range(2):
-                    c = (2 * j + u) * P
-                    nc.tensor.transpose(bank[:, c : c + P], words[:, u : MP // 2 : 2], ident[:])
-            dst = grouped[g][:, half * 1024 : (half + 1) * 1024].bitcast(F32)
+                    nc.tensor.transpose(bank[:, (2 * r + u) * P : (2 * r + u + 1) * P], words[:, u : MP // 2 : 2], identity[:])
             nc.scalar.copy(
-                out=dst.rearrange("p (j r u) -> p j r u", j=2, u=2), in_=bank[:].rearrange("p (j u r) -> p j r u", j=2, u=2)
+                out=h_prev_quads[g][:, pair * 1024 : (pair + 1) * 1024].bitcast(F32).rearrange("p (r n u) -> p r n u", r=2, u=2),
+                in_=bank[:].rearrange("p (r u n) -> p r n u", r=2, u=2),
             )
 
-        def quant_x(g):
+        def quantise_h_prev(g):
             if not 0 <= g < GROUPS:
                 return
-            x_codes = pool.tile([P, TOK], U32, align_bytes=64)
-            x_scales = pool.tile([P, TOK], U8, align_bytes=64)
-            xc[g], xs[g] = x_codes, x_scales
-            nc.vector.quantize_mx(out=x_codes[:].bitcast(FP8X4), scales=x_scales[:], in_=grouped[g][:])
+            n = SUBS[g] * P
+            x_codes = pool.tile([P, n], U32, align_bytes=64)
+            x_scales = pool.tile([P, n], U8, align_bytes=64)
+            h_prev_codes[g], h_prev_scales[g] = x_codes, x_scales
+            nc.vector.quantize_mx(out=x_codes[:].bitcast(FP8X4), scales=x_scales[:], in_=h_prev_quads[g][:])
+
+        def permute_w_hid():
+            for dst, src in ((hid_scales, hid_bytes), (hid_codes, hid_words)):
+                nc.vector.tensor_copy(
+                    out=dst[:].rearrange("p (h t m) -> p h t m", h=2, t=PACK), in_=src[:].rearrange("p (h m t) -> p h t m", h=2, t=PACK)
+                )
 
         def first(g, half, t):
             if not 0 <= g < GROUPS:
                 return
-            if (g, half) not in hp:
-                h_planes = pool.tile([P, 4, TOK], BF16, bufs=3)
-                hp[g, half] = h_planes
-            bank = new_bank()
-            m = slice((4 * half + t) * P, (4 * half + t + 1) * P)
+            n = SUBS[g] * P
+            if (g, half) not in h_planes:
+                planes = pool.tile([P, PACK, n], BF16, bufs=3)
+                h_planes[g, half] = planes
+            bank = work_bank()
+            channels = slice((PACK * half + t) * P, (PACK * half + t + 1) * P)
             nc.tensor.matmul_mx(
-                out=bank[:],
-                lhsT=wh[:, m].bitcast(FP8X4),
-                lhsT_scale=wh_scale[:, m],
-                rhs=xc[g][:].bitcast(FP8X4),
-                rhs_scale=xs[g][:],
+                out=bank[:, 0:n],
+                lhsT=hid_codes[:, channels].bitcast(FP8X4),
+                lhsT_scale=hid_scales[:, channels],
+                rhs=h_prev_codes[g][:].bitcast(FP8X4),
+                rhs_scale=h_prev_scales[g][:],
                 start=True,
                 stop=True,
             )
-            nc.scalar.activation(out=hp[g, half][:, t, :], in_=bank[:], func=RELU, bias=bh[:, half, t : t + 1])
+            nc.scalar.activation(out=h_planes[g, half][:, t, :], in_=bank[:, 0:n], func=RELU, bias=hid_bias[:, half, t : t + 1])
 
         def weave(g, half, on_scalar):
             if not 0 <= g < GROUPS:
                 return
-            if (g, half) not in hg:
-                h_grp = pool.tile([P, TOK, 4], BF16, bufs=3, align_bytes=64)
-                hg[g, half] = h_grp
-            cols = slice(0, N_SCALAR) if on_scalar else slice(N_SCALAR, TOK)
-            dst = hg[g, half][:, cols, :].rearrange("p (c i) t -> p c t i", i=4)
-            src = hp[g, half][:, :, cols].rearrange("p t (c i) -> p c t i", i=4)
-            if on_scalar:
-                nc.scalar.copy(out=dst, in_=src)
-            else:
-                nc.vector.tensor_copy(out=dst, in_=src)
+            n = SUBS[g] * P
+            if (g, half) not in h_quads:
+                quads_h = pool.tile([P, n, PACK], BF16, bufs=3, align_bytes=64)
+                h_quads[g, half] = quads_h
+            share = SCALAR_COLUMNS[g]
+            columns = slice(0, share) if on_scalar else slice(share, n)
+            copy = nc.scalar.copy if on_scalar else nc.vector.tensor_copy
+            copy(
+                out=h_quads[g, half][:, columns, :].rearrange("p (c i) t -> p c t i", i=4),
+                in_=h_planes[g, half][:, :, columns].rearrange("p t (c i) -> p c t i", i=4),
+            )
 
-        def quant_h(g, half):
+        def quantise_h(g, half):
             if not 0 <= g < GROUPS:
                 return
-            h_codes = pool.tile([P, TOK], U32, bufs=4, align_bytes=64)
-            h_scales = pool.tile([P, TOK], U8, bufs=4, align_bytes=64)
-            hc[g, half], hs[g, half] = h_codes, h_scales
-            nc.vector.quantize_mx(
-                out=h_codes[:].bitcast(FP8X4), scales=h_scales[:], in_=hg[g, half][:].rearrange("p n t -> p (n t)")
-            )
+            n = SUBS[g] * P
+            codes = pool.tile([P, n], U32, bufs=4, align_bytes=64)
+            scales = pool.tile([P, n], U8, bufs=4, align_bytes=64)
+            h_codes[g, half], h_scales[g, half] = codes, scales
+            nc.vector.quantize_mx(out=codes[:].bitcast(FP8X4), scales=scales[:], in_=h_quads[g, half][:].rearrange("p n t -> p (n t)"))
 
         def second(g, c):
             if not 0 <= g < GROUPS:
                 return
-            if g not in st:
-                shift_t = pool.tile([P, 3, TOK], F32)
-                st[g] = shift_t
-            bank = new_bank()
+            n = SUBS[g] * P
+            if g not in shift:
+                shift_g = pool.tile([P, C_TILES, n], F32)
+                shift[g] = shift_g
+            bank = work_bank()
+            channels = slice(c * P, (c + 1) * P)
             for half in range(2):
                 nc.tensor.matmul_mx(
-                    out=bank[:],
-                    lhsT=wo[:, half, c * P : (c + 1) * P].bitcast(FP8X4),
-                    lhsT_scale=wo_scale[:, half, c * P : (c + 1) * P],
-                    rhs=hc[g, half][:].bitcast(FP8X4),
-                    rhs_scale=hs[g, half][:],
+                    out=bank[:, 0:n],
+                    lhsT=out_codes[:, half, channels].bitcast(FP8X4),
+                    lhsT_scale=out_scales[:, half, channels],
+                    rhs=h_codes[g, half][:].bitcast(FP8X4),
+                    rhs_scale=h_scales[g, half][:],
                     start=(half == 0),
                     stop=(half == 1),
                 )
-            nc.scalar.activation(out=st[g][:, c, :], in_=bank[:], func=IDENTITY, bias=bo[:, c, 0:1])
+            nc.scalar.activation(out=shift[g][:, c, :], in_=bank[:, 0:n], func=IDENTITY, bias=out_bias[:, c, 0:1])
 
-        uses = []
-        for pair in range(2):
-            a, b = 2 * pair, 2 * pair + 1
-            uses.append(((a, 0), (a, 1)))
-            uses.append(((a, 2), (b, 2)))
-            uses.append(((b, 0), (b, 1)))
+        uses = (((0, 0), (0, 1)), ((0, 2), (1, 2)), ((1, 0), (1, 1)))
 
         def turn_back(g, n):
-            if not 0 <= g < GROUPS:
+            if not 0 <= g < GROUPS or n // 3 >= SUBS[g] // 2:
                 return
-            for s in range(2):
-                j, c = uses[n][s]
+            for s, (r, c) in enumerate(uses[n % 3]):
+                tokens = slice((2 * (n // 3) + r) * P, (2 * (n // 3) + r + 1) * P)
                 nc.tensor.transpose(
-                    mix[n % MIX][:, 256 + s * P : 256 + (s + 1) * P], st[g][:, c, j * P : (j + 1) * P], ident[:]
+                    couple_banks[n % 3 % COUPLE_BANKS][:, 256 + s * P : 256 + (s + 1) * P], shift[g][:, c, tokens], identity[:]
                 )
 
         def couple(g, n):
-            if not 0 <= g < GROUPS:
+            if not 0 <= g < GROUPS or n // 3 >= SUBS[g] // 2:
                 return
-            pair = n // 3
-            if n % 3 == 0:
-                y_pair = pool.tile([P, 2, D], F32, bufs=3)
-                yo[g, pair] = y_pair
-            y = yo[g, pair]
-            xi = x_in[g][:, 2 * pair : 2 * pair + 2, :]
-            bank = mix[n % MIX]
-            if n % 3 == 1:
-                nc.vector.tensor_tensor(
-                    out=y[:, :, 512:768].rearrange("p q (n e) -> p q n e", e=2),
-                    in0=bank[:].rearrange("p (e q n) -> p q n e", e=2, q=2),
-                    in1=xi[:, :, 512:768].rearrange("p q (n e) -> p q n e", e=2),
-                    op=ADD,
-                )
+            pair, use = n // 3, n % 3
+            if use == 0:
+                y_pair = pool.tile([P, 2, D], F32, bufs=6)
+                y[g, pair] = y_pair
+            x_pair = x_rows[g][:, 2 * pair : 2 * pair + 2, :]
+            bank = couple_banks[use % COUPLE_BANKS]
+            if use == 1:
+                view = lambda a: a[:, :, 512:768].rearrange("p r (n e) -> p r n e", e=2)
+                bank_view = bank[:].rearrange("p (e r n) -> p r n e", e=2, r=2)
             else:
-                q = 0 if n % 3 == 0 else 1
-                nc.vector.tensor_tensor(
-                    out=y[:, q, 0:512].rearrange("p (n e) -> p n e", e=2),
-                    in0=bank[:].rearrange("p (e n) -> p n e", e=2),
-                    in1=xi[:, q, 0:512].rearrange("p (n e) -> p n e", e=2),
-                    op=ADD,
-                )
-            if n % 3 == 2:
-                rows = out[g * TOK : (g + 1) * TOK, :].rearrange("(p j) d -> p j d", j=SUB)
-                nc.sync.dma_start(out=rows[:, 2 * pair : 2 * pair + 2, :], in_=y[:])
+                view = lambda a: a[:, use // 2, 0:512].rearrange("p (n e) -> p n e", e=2)
+                bank_view = bank[:].rearrange("p (e n) -> p n e", e=2)
+            nc.vector.tensor_tensor(out=view(y[g, pair]), in0=bank_view, in1=view(x_pair), op=ADD)
+            if use > 0:
+                r = use - 1
+                nc.sync.dma_start(out=rows_of(out, g)[:, 2 * pair + r, :], in_=y[g, pair][:, r, :])
 
-        def prepare(g):
-            if g != 0:
-                return
-            nc.vector.tensor_copy(out=k_scale[:, 1, :], in_=k_scale[:, 0, :])
-            nc.vector.tensor_copy(out=wh_scale[:].rearrange("p (h t m) -> p h t m", h=2, t=4), in_=wh_scale_raw[:].rearrange("p (h m t) -> p h t m", h=2, t=4))
-            nc.vector.tensor_copy(out=wh[:].rearrange("p (h t m) -> p h t m", h=2, t=4), in_=wh_raw[:].rearrange("p (h m t) -> p h t m", h=2, t=4))
-
-        for i in range(-6, GROUPS + 4):
+        widen(0)
+        for pair in range(SUBS[0] // 2):
+            turn(0, pair)
+        permute_w_hid()
+        quantise_h_prev(0)
+        widen(1)
+        widened = 2
+        for i in range(GROUPS + 3):
+            turn_back(i - 3, 0)
+            second(i - 2, 2)
+            turn_back(i - 3, 1)
             first(i, 0, 0)
+            couple(i - 3, 0)
             first(i, 0, 1)
-            first(i, 0, 2)
-            first(i, 0, 3)
-            first(i, 1, 0)
-            widen(i + 4, 0)
-            turn_back(i - 2, 0)
-            turn_back(i - 2, 1)
-            first(i, 1, 3)
-            second(i - 1, 0)
-            first(i, 1, 1)
-            couple(i - 2, 0)
-            turn_back(i - 2, 2)
-            turn(i + 2, 1)
-            couple(i - 2, 1)
             first(i, 1, 2)
-            weave(i, 0, True)
-            couple(i - 2, 2)
-            weave(i, 1, True)
-            weave(i, 0, False)
+            first(i, 1, 1)
+            first(i, 0, 3)
+            couple(i - 3, 1)
+            turn_back(i - 3, 2)
+            couple(i - 3, 2)
+            ahead = min(GROUPS, widened + (2 if i in (1, 2) else 1))
+            for g in range(widened, ahead):
+                widen(g)
+            widened = ahead
+            turn(i + 1, 0)
+            turn(i + 1, 1)
             turn_back(i - 2, 3)
-            second(i - 1, 1)
             couple(i - 2, 3)
+            first(i, 0, 2)
+            first(i, 1, 0)
             turn_back(i - 2, 4)
             turn_back(i - 2, 5)
             couple(i - 2, 4)
-            quant_x(i + 2)
             couple(i - 2, 5)
+            first(i, 1, 3)
+            weave(i, 0, True)
+            quantise_h_prev(i + 1)
+            weave(i, 0, False)
+            weave(i, 1, True)
             weave(i, 1, False)
-            turn(i + 3, 0)
-            widen(i + 4, 1)
-            prepare(i + 4)
-            second(i - 1, 2)
-            quant_h(i, 0)
-            quant_h(i, 1)
+            second(i - 1, 0)
+            quantise_h(i, 0)
+            second(i - 1, 1)
+            quantise_h(i, 1)

from contextlib import ExitStack

import concourse.mybir as mybir
from concourse.masks import make_identity

B, D, MP, MID = 4096, 768, 512, 1024
HALF = D // 2
FLOPS = 2 * B * (MP * MID + MID * HALF)

F32 = mybir.dt.float32
BF16 = mybir.dt.bfloat16
U8 = mybir.dt.uint8
U32 = mybir.dt.uint32
I32 = mybir.dt.int32
FP8 = mybir.dt.float8_e4m3fn
FP8X4 = mybir.dt.float8_e4m3fn_x4
ADD = mybir.AluOpType.add
MULT = mybir.AluOpType.mult
RELU = mybir.ActivationFunctionType.Relu
IDENTITY = mybir.ActivationFunctionType.Identity

P = 128
PACK = 4
SUBS = [2, 4, 4, 4, 4, 4, 4, 4, 2]
FIRST_TOKEN = [P * sum(SUBS[:g]) for g in range(len(SUBS))]
GROUPS = len(SUBS)
C_TILES = HALF // P
COUPLE_BANKS = 3
WORK_BANKS = 8 - COUPLE_BANKS
SCALAR_COLUMNS = [64, 128, 128, 128, 128, 128, 128, 128, 96]
LOOKAHEAD = 3


def tile_additivecoupling_pa_t_w8_kernel(
    tc, x, h_prev_bytes, h_prev_scale, w_hid_words, w_hid_scales, b_hid, w_out_words, w_out_scales, b_out, out
):
    nc = tc.nc
    with ExitStack() as ctx:
        keep = ctx.enter_context(tc.tile_pool(name="keep", bufs=1))
        pool = ctx.enter_context(tc.tile_pool(name="pool", bufs=2))
        work = ctx.enter_context(tc.psum_pool(name="work", bufs=WORK_BANKS))
        fixed = ctx.enter_context(tc.psum_pool(name="fixed", bufs=1))
        ctx.enter_context(tc.manual_schedule())

        h_bytes = [keep.tile([P, SUBS[g] * MP], U8, name="h_bytes%d" % g, align_bytes=64) for g in range(GROUPS)]
        x_rows = [keep.tile([P, SUBS[g], D], BF16, name="x_rows%d" % g) for g in range(GROUPS)]
        k_column = keep.tile([P, PACK], F32)
        k_scale = keep.tile([P, max(SUBS), MP], F32)
        hid_words = keep.tile([P, MID], I32)
        hid_bytes = keep.tile([P, MID], U8, align_bytes=64)
        hid_codes = keep.tile([P, MID], I32, align_bytes=64)
        hid_scales = keep.tile([P, MID], U8, align_bytes=64)
        out_codes = keep.tile([P, 2, HALF], I32, align_bytes=64)
        out_scales = keep.tile([P, 2, HALF], U8, align_bytes=64)
        hid_bias = keep.tile([P, 2, PACK], BF16)
        out_bias = keep.tile([P, C_TILES, 2], BF16)
        zeros = keep.tile([P, 256], BF16)
        identity = keep.tile([P, P], F32)

        def rows_of(tensor, g):
            n = SUBS[g] * P
            return tensor[FIRST_TOKEN[g] : FIRST_TOKEN[g] + n, :].rearrange("(p r) d -> p r d", r=SUBS[g])

        def load_bytes(g):
            nc.sync.dma_start(out=h_bytes[g][:], in_=rows_of(h_prev_bytes, g).rearrange("p r k -> p (r k)"))

        def load_x(g):
            nc.sync.dma_start(out=x_rows[g][:], in_=rows_of(x, g))

        def load_words(tile_view, words):
            nc.sync.dma_start(out=tile_view, in_=words.rearrange("p n t -> p (n t)").bitcast(I32))

        def load_scales(tile_view, scales):
            for q in range(4):
                nc.sync.dma_start(
                    out=tile_view[32 * q : 32 * q + 4, :].bitcast(I32), in_=scales[4 * q : 4 * q + 4, :].bitcast(I32)
                )

        nc.vector.memset(hid_bytes[:].bitcast(I32), 0)
        nc.vector.memset(out_scales[:].rearrange("p g n -> p (g n)").bitcast(I32), 0)
        nc.vector.memset(zeros[:], 0.0)
        make_identity(nc, identity[:])

        nc.scalar.dma_start(out=k_column[:], in_=h_prev_scale.rearrange("o (p t) -> p (o t)", t=PACK))
        nc.scalar.dma_start(out=hid_bias[:], in_=b_hid.rearrange("(h p t) -> p h t", h=2, t=PACK))
        nc.scalar.dma_start(out=out_bias[:, :, 0:1], in_=b_out.rearrange("(c p o) -> p c o", p=P, o=1))
        load_bytes(0)
        load_bytes(1)
        load_scales(hid_bytes, w_hid_scales[0])
        load_words(hid_words[:], w_hid_words[0])
        load_bytes(2)
        load_bytes(3)
        for g in range(2):
            load_scales(out_scales[:, g, :], w_out_scales[g])
        for g in range(2):
            load_words(out_codes[:, g, :], w_out_words[g])
        for g in range(GROUPS):
            load_x(g)
            if g + LOOKAHEAD + 1 < GROUPS:
                load_bytes(g + LOOKAHEAD + 1)

        couple_banks = [fixed.tile([P, 512], F32, name="couple_bank%d" % d) for d in range(COUPLE_BANKS)]
        for bank in couple_banks:
            nc.tensor.matmul(out=bank[:, 0:256], lhsT=zeros[:, 0:P], rhs=zeros[:], start=True, stop=True)

        def work_bank():
            bank = work.tile([P, 512], F32)
            return bank

        scale_bank = work_bank()
        for t in range(PACK):
            nc.tensor.transpose(scale_bank[:, t * P : (t + 1) * P], k_column[:, t : t + 1].to_broadcast([P, P]), identity[:])
        for r in range(max(SUBS)):
            copy = nc.vector.tensor_copy if r == 0 else nc.scalar.copy
            copy(out=k_scale[:, r, :].rearrange("p (n t) -> p n t", t=PACK), in_=scale_bank[:].rearrange("p (t n) -> p n t", t=PACK))

        h_prev, h_prev_quads, h_prev_codes, h_prev_scales = {}, {}, {}, {}
        h_planes, h_quads, h_codes, h_scales, shift, y = {}, {}, {}, {}, {}, {}

        def widen(g):
            width = SUBS[g] * MP
            h_wide = pool.tile([P, width], BF16, bufs=4)
            h_prev[g] = h_wide
            step = MP if g == 0 else width
            for c in range(0, width, step):
                nc.vector.tensor_tensor(
                    out=h_wide[:, c : c + step],
                    in0=h_bytes[g][:, c : c + step].bitcast(FP8),
                    in1=k_scale[:].rearrange("p r k -> p (r k)")[:, 0:step],
                    op=MULT,
                )

        def turn(g, pair):
            if not 0 <= g < GROUPS or 2 * pair >= SUBS[g]:
                return
            if g not in h_prev_quads:
                quads = pool.tile([P, SUBS[g] * P * PACK], BF16, align_bytes=64)
                h_prev_quads[g] = quads
            bank = work_bank()
            for r in range(2):
                words = h_prev[g][:, (2 * pair + r) * MP : (2 * pair + r + 1) * MP].bitcast(F32)
                for u in range(2):
                    nc.tensor.transpose(bank[:, (2 * r + u) * P : (2 * r + u + 1) * P], words[:, u : MP // 2 : 2], identity[:])
            nc.scalar.copy(
                out=h_prev_quads[g][:, pair * 1024 : (pair + 1) * 1024].bitcast(F32).rearrange("p (r n u) -> p r n u", r=2, u=2),
                in_=bank[:].rearrange("p (r u n) -> p r n u", r=2, u=2),
            )

        def quantise_h_prev(g):
            if not 0 <= g < GROUPS:
                return
            n = SUBS[g] * P
            x_codes = pool.tile([P, n], U32, align_bytes=64)
            x_scales = pool.tile([P, n], U8, align_bytes=64)
            h_prev_codes[g], h_prev_scales[g] = x_codes, x_scales
            nc.vector.quantize_mx(out=x_codes[:].bitcast(FP8X4), scales=x_scales[:], in_=h_prev_quads[g][:])

        def permute_w_hid():
            for dst, src in ((hid_scales, hid_bytes), (hid_codes, hid_words)):
                nc.vector.tensor_copy(
                    out=dst[:].rearrange("p (h t m) -> p h t m", h=2, t=PACK), in_=src[:].rearrange("p (h m t) -> p h t m", h=2, t=PACK)
                )

        def first(g, half, t):
            if not 0 <= g < GROUPS:
                return
            n = SUBS[g] * P
            if (g, half) not in h_planes:
                planes = pool.tile([P, PACK, n], BF16, bufs=3)
                h_planes[g, half] = planes
            bank = work_bank()
            channels = slice((PACK * half + t) * P, (PACK * half + t + 1) * P)
            nc.tensor.matmul_mx(
                out=bank[:, 0:n],
                lhsT=hid_codes[:, channels].bitcast(FP8X4),
                lhsT_scale=hid_scales[:, channels],
                rhs=h_prev_codes[g][:].bitcast(FP8X4),
                rhs_scale=h_prev_scales[g][:],
                start=True,
                stop=True,
            )
            nc.scalar.activation(out=h_planes[g, half][:, t, :], in_=bank[:, 0:n], func=RELU, bias=hid_bias[:, half, t : t + 1])

        def weave(g, half, on_scalar):
            if not 0 <= g < GROUPS:
                return
            n = SUBS[g] * P
            if (g, half) not in h_quads:
                quads_h = pool.tile([P, n, PACK], BF16, bufs=3, align_bytes=64)
                h_quads[g, half] = quads_h
            share = SCALAR_COLUMNS[g]
            columns = slice(0, share) if on_scalar else slice(share, n)
            copy = nc.scalar.copy if on_scalar else nc.vector.tensor_copy
            copy(
                out=h_quads[g, half][:, columns, :].rearrange("p (c i) t -> p c t i", i=4),
                in_=h_planes[g, half][:, :, columns].rearrange("p t (c i) -> p c t i", i=4),
            )

        def quantise_h(g, half):
            if not 0 <= g < GROUPS:
                return
            n = SUBS[g] * P
            codes = pool.tile([P, n], U32, bufs=4, align_bytes=64)
            scales = pool.tile([P, n], U8, bufs=4, align_bytes=64)
            h_codes[g, half], h_scales[g, half] = codes, scales
            nc.vector.quantize_mx(out=codes[:].bitcast(FP8X4), scales=scales[:], in_=h_quads[g, half][:].rearrange("p n t -> p (n t)"))

        def second(g, c):
            if not 0 <= g < GROUPS:
                return
            n = SUBS[g] * P
            if g not in shift:
                shift_g = pool.tile([P, C_TILES, n], F32)
                shift[g] = shift_g
            bank = work_bank()
            channels = slice(c * P, (c + 1) * P)
            for half in range(2):
                nc.tensor.matmul_mx(
                    out=bank[:, 0:n],
                    lhsT=out_codes[:, half, channels].bitcast(FP8X4),
                    lhsT_scale=out_scales[:, half, channels],
                    rhs=h_codes[g, half][:].bitcast(FP8X4),
                    rhs_scale=h_scales[g, half][:],
                    start=(half == 0),
                    stop=(half == 1),
                )
            nc.scalar.activation(out=shift[g][:, c, :], in_=bank[:, 0:n], func=IDENTITY, bias=out_bias[:, c, 0:1])

        uses = (((0, 0), (0, 1)), ((0, 2), (1, 2)), ((1, 0), (1, 1)))

        def turn_back(g, n):
            if not 0 <= g < GROUPS or n // 3 >= SUBS[g] // 2:
                return
            for s, (r, c) in enumerate(uses[n % 3]):
                tokens = slice((2 * (n // 3) + r) * P, (2 * (n // 3) + r + 1) * P)
                nc.tensor.transpose(
                    couple_banks[n % 3 % COUPLE_BANKS][:, 256 + s * P : 256 + (s + 1) * P], shift[g][:, c, tokens], identity[:]
                )

        def couple(g, n):
            if not 0 <= g < GROUPS or n // 3 >= SUBS[g] // 2:
                return
            pair, use = n // 3, n % 3
            if use == 0:
                y_pair = pool.tile([P, 2, D], F32, bufs=6)
                y[g, pair] = y_pair
            x_pair = x_rows[g][:, 2 * pair : 2 * pair + 2, :]
            bank = couple_banks[use % COUPLE_BANKS]
            if use == 1:
                view = lambda a: a[:, :, 512:768].rearrange("p r (n e) -> p r n e", e=2)
                bank_view = bank[:].rearrange("p (e r n) -> p r n e", e=2, r=2)
            else:
                view = lambda a: a[:, use // 2, 0:512].rearrange("p (n e) -> p n e", e=2)
                bank_view = bank[:].rearrange("p (e n) -> p n e", e=2)
            nc.vector.tensor_tensor(out=view(y[g, pair]), in0=bank_view, in1=view(x_pair), op=ADD)
            if use > 0:
                r = use - 1
                nc.sync.dma_start(out=rows_of(out, g)[:, 2 * pair + r, :], in_=y[g, pair][:, r, :])

        widen(0)
        for pair in range(SUBS[0] // 2):
            turn(0, pair)
        permute_w_hid()
        quantise_h_prev(0)
        widen(1)
        widened = 2
        for i in range(GROUPS + 3):
            turn_back(i - 3, 0)
            second(i - 2, 2)
            turn_back(i - 3, 1)
            first(i, 0, 0)
            couple(i - 3, 0)
            first(i, 0, 1)
            first(i, 1, 2)
            first(i, 1, 1)
            first(i, 0, 3)
            couple(i - 3, 1)
            turn_back(i - 3, 2)
            couple(i - 3, 2)
            ahead = min(GROUPS, widened + (2 if i in (1, 2) else 1))
            for g in range(widened, ahead):
                widen(g)
            widened = ahead
            turn(i + 1, 0)
            turn(i + 1, 1)
            turn_back(i - 2, 3)
            couple(i - 2, 3)
            first(i, 0, 2)
            first(i, 1, 0)
            turn_back(i - 2, 4)
            turn_back(i - 2, 5)
            couple(i - 2, 4)
            couple(i - 2, 5)
            first(i, 1, 3)
            weave(i, 0, True)
            quantise_h_prev(i + 1)
            weave(i, 0, False)
            weave(i, 1, True)
            weave(i, 1, False)
            second(i - 1, 0)
            quantise_h(i, 0)
            second(i - 1, 1)
            quantise_h(i, 1)
